import numpy as np
import ml_dtypes

BF16 = ml_dtypes.bfloat16


def bf(x):
    return np.asarray(x, np.float32).astype(BF16)


def f32(x):
    return np.asarray(x, np.float32)


def f64(x):
    return np.asarray(x).astype(np.float64)


def striped(idx):
    return np.tile(idx.reshape(-1, 16).T, (8, 1))


C, S, N, L = 128, 4096, 2304, 4
R = np.sqrt(0.5)
LEN = [S >> (k + 1) for k in range(L)] + [S >> L]
REV = LEN[::-1]


def wavedec(y):
    details = []
    cur = y
    for _ in range(L):
        p = cur.reshape(cur.shape[0], -1, 2)
        details.append((p[..., 0] - p[..., 1]) * R)
        cur = (p[..., 0] + p[..., 1]) * R
    return np.concatenate([cur] + details[::-1], axis=-1)


def waverec(parts):
    a = parts[0]
    for d in parts[1:]:
        a = np.stack([(a + d) * R, (a - d) * R], axis=-1).reshape(a.shape[0], -1)
    return a


def setup_inputs():
    return {"x": f32(np.random.standard_normal((C, S))), "pre": f32(np.random.standard_normal((1, S))), "mid": f32(np.random.standard_normal((1, N))), "post": f32(np.random.standard_normal((1, S))), "offs": striped(np.random.permutation(S)[:N])}


def reference(x, pre, mid, post, offs):
    idx = offs[:16].T.reshape(-1)
    w = wavedec(f64(x) * f64(pre))
    t = w[:, idx] * f64(mid)
    parts = []
    start = 0
    for k in range(L + 1):
        parts.append(t[:, start:start + REV[k]])
        start = LEN[k]
    return waverec(parts) * f64(post)

@@ -1,0 +1,106 @@
+import math
+
+import concourse.mybir as mybir
+
+F32 = mybir.dt.float32
+U16 = mybir.dt.uint16
+ADD = mybir.AluOpType.add
+SUB = mybir.AluOpType.subtract
+MULT = mybir.AluOpType.mult
+
+P = 128
+S = 4096
+N = 2304
+R = math.sqrt(0.5)
+ROOT = S // 16
+
+IN_CHUNKS = 4
+IN_COLS = S // IN_CHUNKS
+OUT_CHUNKS = 4
+OUT_ROOTS = ROOT // OUT_CHUNKS
+
+
+def pairs(ap):
+    two = ap.rearrange("p (n two) -> p n two", two=2)
+    return two[:, :, 0], two[:, :, 1]
+
+
+def tile_waveletlayer_kernel(tc, x, pre, mid, post, offs, out):
+    nc = tc.nc
+    pre_row = pre.rearrange("o n -> (o n)")
+    mid_row = mid.rearrange("o n -> (o n)")
+    post_row = post.rearrange("o n -> (o n)")
+
+    with tc.tile_pool(name="held", bufs=1) as held:
+        offsets = held.tile([P, N // 16], U16, name="offsets")
+        nc.sync.dma_start(offsets[:], offs)
+        x_sb = held.tile([P, S], F32, name="x_sb")
+        pre_sb = held.tile([P, S], F32, name="pre_sb")
+        mid_sb = held.tile([P, N], F32, name="mid_sb")
+        post_sb = held.tile([P, S], F32, name="post_sb")
+        for c in range(IN_CHUNKS):
+            cols = slice(c * IN_COLS, (c + 1) * IN_COLS)
+            nc.sync.dma_start(x_sb[:, cols], x[:, cols])
+            nc.scalar.dma_start(pre_sb[:, cols], pre_row[cols].partition_broadcast(P))
+        nc.sync.dma_start(mid_sb[:], mid_row.partition_broadcast(P))
+        nc.scalar.dma_start(post_sb[:], post_row.partition_broadcast(P))
+
+        y = held.tile([P, S], F32, name="y")
+        sums = {0: y}
+        diffs = {}
+        for k in (1, 2, 3):
+            sums[k] = held.tile([P, S >> k], F32, name=f"sum{k}")
+            diffs[k] = held.tile([P, S >> k], F32, name=f"diff{k}")
+        w = held.tile([P, S], F32, name="w")
+        for c in range(IN_CHUNKS):
+            cols = slice(c * IN_COLS, (c + 1) * IN_COLS)
+            nc.vector.scalar_tensor_tensor(y[:, cols], x_sb[:, cols], R**4, pre_sb[:, cols], MULT, MULT)
+            for k in (1, 2, 3, 4):
+                wide = IN_COLS >> (k - 1)
+                half = IN_COLS >> k
+                even, odd = pairs(sums[k - 1][:, c * wide : (c + 1) * wide])
+                here = slice(c * half, (c + 1) * half)
+                in_w = slice((S >> k) + c * half, (S >> k) + (c + 1) * half)
+                if k < 4:
+                    nc.vector.tensor_tensor(sums[k][:, here], even, odd, ADD)
+                    nc.vector.tensor_tensor(diffs[k][:, here], even, odd, SUB)
+                    nc.scalar.mul(w[:, in_w], diffs[k][:, here], R ** (k - 4))
+                else:
+                    nc.vector.tensor_tensor(w[:, here], even, odd, ADD)
+                    nc.vector.tensor_tensor(w[:, in_w], even, odd, SUB)
+
+        t = held.tile([P, N], F32, name="t")
+        nc.vector.tensor_tensor(t[:], w[:].indirect(offsets[:]), mid_sb[:], MULT)
+
+        starts = {1: 2048, 2: 1024, 3: 512, 4: 256}
+        z = {0: t[:, 0:ROOT]}
+        for k in (1, 2, 3, 4):
+            z[k] = held.tile([P, ROOT << k], F32, name=f"z{k}")
+
+        def level(k, roots):
+            b = 1 << (k - 1)
+            f_k = t[:, starts[k] : starts[k] + ROOT * b].rearrange("p (m b) -> p b m", b=b)
+            below = z[k - 1].rearrange("p (b m) -> p b m", b=b)
+            above = z[k].rearrange("p (b s m) -> p b s m", b=b, s=2)
+            for s, sign in ((0, 1.0), (1, -1.0)):
+                nc.vector.scalar_tensor_tensor(
+                    above[:, :, s, roots], f_k[:, :, roots], sign * R ** (1 - k), below[:, :, roots], MULT, ADD
+                )
+
+        for k in (1, 2, 3):
+            level(k, slice(0, ROOT))
+        o_sb = held.tile([P, S], F32, name="o_sb")
+        sorted_back = z[4].rearrange("p (b m) -> p m b", b=16)
+        for c in range(OUT_CHUNKS):
+            roots = slice(c * OUT_ROOTS, (c + 1) * OUT_ROOTS)
+            cols = slice(c * OUT_ROOTS * 16, (c + 1) * OUT_ROOTS * 16)
+            level(4, roots)
+            nc.vector.scalar_tensor_tensor(
+                o_sb[:, cols].rearrange("p (m b) -> p m b", b=16),
+                sorted_back[:, roots, :],
+                R**4,
+                post_sb[:, cols].rearrange("p (m b) -> p m b", b=16),
+                MULT,
+                MULT,
+            )
+            nc.sync.dma_start(out[:, cols], o_sb[:, cols])

@@ -13,16 +13,20 @@ S = 4096
 N = 2304
 R = math.sqrt(0.5)
 ROOT = S // 16
+F_START = {1: 2048, 2: 1024, 3: 512, 4: 256}
+SIGNS = ((0, 1.0), (1, -1.0))
 
-IN_CHUNKS = 4
-IN_COLS = S // IN_CHUNKS
+IN_CHUNKS = 8
 OUT_CHUNKS = 4
 OUT_ROOTS = ROOT // OUT_CHUNKS
 
 
-def pairs(ap):
-    two = ap.rearrange("p (n two) -> p n two", two=2)
-    return two[:, :, 0], two[:, :, 1]
+def grouped(ap, g):
+    return ap.rearrange("p (j r) -> p j r", r=g)
+
+
+def across(ap, runs):
+    return ap.rearrange("p (r j) -> p j r", r=runs)
 
 
 def tile_waveletlayer_kernel(tc, x, pre, mid, post, offs, out):
@@ -39,68 +43,101 @@ def tile_waveletlayer_kernel(tc, x, pre, mid, post, offs, out):
         mid_sb = held.tile([P, N], F32, name="mid_sb")
         post_sb = held.tile([P, S], F32, name="post_sb")
         for c in range(IN_CHUNKS):
-            cols = slice(c * IN_COLS, (c + 1) * IN_COLS)
+            cols = slice(c * (S // IN_CHUNKS), (c + 1) * (S // IN_CHUNKS))
             nc.sync.dma_start(x_sb[:, cols], x[:, cols])
             nc.scalar.dma_start(pre_sb[:, cols], pre_row[cols].partition_broadcast(P))
         nc.sync.dma_start(mid_sb[:], mid_row.partition_broadcast(P))
         nc.scalar.dma_start(post_sb[:], post_row.partition_broadcast(P))
 
-        y = held.tile([P, S], F32, name="y")
-        sums = {0: y}
+        sums = {0: held.tile([P, S], F32, name="y")}
         diffs = {}
         for k in (1, 2, 3):
             sums[k] = held.tile([P, S >> k], F32, name=f"sum{k}")
             diffs[k] = held.tile([P, S >> k], F32, name=f"diff{k}")
         w = held.tile([P, S], F32, name="w")
-        for c in range(IN_CHUNKS):
-            cols = slice(c * IN_COLS, (c + 1) * IN_COLS)
-            nc.vector.scalar_tensor_tensor(y[:, cols], x_sb[:, cols], R**4, pre_sb[:, cols], MULT, MULT)
-            for k in (1, 2, 3, 4):
-                wide = IN_COLS >> (k - 1)
-                half = IN_COLS >> k
-                even, odd = pairs(sums[k - 1][:, c * wide : (c + 1) * wide])
-                here = slice(c * half, (c + 1) * half)
-                in_w = slice((S >> k) + c * half, (S >> k) + (c + 1) * half)
-                if k < 4:
-                    nc.vector.tensor_tensor(sums[k][:, here], even, odd, ADD)
-                    nc.vector.tensor_tensor(diffs[k][:, here], even, odd, SUB)
-                    nc.scalar.mul(w[:, in_w], diffs[k][:, here], R ** (k - 4))
-                else:
-                    nc.vector.tensor_tensor(w[:, here], even, odd, ADD)
-                    nc.vector.tensor_tensor(w[:, in_w], even, odd, SUB)
+
+        def scale(part, parts):
+            cols = slice(part * (S // parts), (part + 1) * (S // parts))
+            nc.vector.scalar_tensor_tensor(sums[0][:, cols], x_sb[:, cols], R**4, pre_sb[:, cols], MULT, MULT)
+
+        def analyse(k, part, parts):
+            half = (S >> k) // parts
+            two = grouped(sums[k - 1][:, 2 * part * half : 2 * (part + 1) * half], 2)
+            even, odd = two[:, :, 0], two[:, :, 1]
+            here = slice(part * half, (part + 1) * half)
+            in_w = slice((S >> k) + part * half, (S >> k) + (part + 1) * half)
+            if k < 4:
+                nc.vector.tensor_tensor(sums[k][:, here], even, odd, ADD)
+                nc.vector.tensor_tensor(diffs[k][:, here], even, odd, SUB)
+                nc.scalar.mul(w[:, in_w], diffs[k][:, here], R ** (k - 4))
+            else:
+                nc.vector.tensor_tensor(w[:, here], even, odd, ADD)
+                nc.vector.tensor_tensor(w[:, in_w], even, odd, SUB)
+
+        for c in range(IN_CHUNKS + 1):
+            if c < IN_CHUNKS:
+                scale(c, IN_CHUNKS)
+            if c > 0:
+                analyse(2, c - 1, IN_CHUNKS)
+            if c < IN_CHUNKS:
+                analyse(1, c, IN_CHUNKS)
+        analyse(3, 0, 1)
+        analyse(4, 0, 1)
 
         t = held.tile([P, N], F32, name="t")
         nc.vector.tensor_tensor(t[:], w[:].indirect(offsets[:]), mid_sb[:], MULT)
 
-        starts = {1: 2048, 2: 1024, 3: 512, 4: 256}
-        z = {0: t[:, 0:ROOT]}
-        for k in (1, 2, 3, 4):
-            z[k] = held.tile([P, ROOT << k], F32, name=f"z{k}")
+        halves = {k: held.tile([P, ROOT << k], F32, name=f"halves{k}") for k in (1, 3)}
+        quarters = {k: held.tile([P, ROOT << k], F32, name=f"quarters{k}") for k in (2, 4)}
+        in_order = {0: grouped(t[:, 0:ROOT], 1), 2: across(quarters[2], 4), 4: across(quarters[4], 4)}
 
-        def level(k, roots):
-            b = 1 << (k - 1)
-            f_k = t[:, starts[k] : starts[k] + ROOT * b].rearrange("p (m b) -> p b m", b=b)
-            below = z[k - 1].rearrange("p (b m) -> p b m", b=b)
-            above = z[k].rearrange("p (b s m) -> p b s m", b=b, s=2)
-            for s, sign in ((0, 1.0), (1, -1.0)):
+        def odd_level(k, m0, m1):
+            g = 1 << (k - 1)
+            n = ROOT * g
+            f_k = t[:, F_START[k] + g * m0 : F_START[k] + g * m1]
+            for s, sign in SIGNS:
                 nc.vector.scalar_tensor_tensor(
-                    above[:, :, s, roots], f_k[:, :, roots], sign * R ** (1 - k), below[:, :, roots], MULT, ADD
+                    grouped(halves[k][:, s * n + g * m0 : s * n + g * m1], g),
+                    grouped(f_k, g),
+                    sign * R ** (1 - k),
+                    in_order[k - 1][:, m0:m1, :],
+                    MULT,
+                    ADD,
                 )
 
-        for k in (1, 2, 3):
-            level(k, slice(0, ROOT))
+        def even_level(k, m0, m1):
+            g = 1 << (k - 2)
+            f_k = t[:, F_START[k] + 2 * g * m0 : F_START[k] + 2 * g * m1]
+            by_sign = quarters[k].rearrange("p (s1 s2 j) -> p s2 j s1", s1=2, s2=2)
+            for s, sign in SIGNS:
+                nc.vector.scalar_tensor_tensor(
+                    by_sign[:, s, g * m0 : g * m1, :],
+                    grouped(f_k, 2),
+                    sign * R ** (1 - k),
+                    across(halves[k - 1], 2)[:, g * m0 : g * m1, :],
+                    MULT,
+                    ADD,
+                )
+
         o_sb = held.tile([P, S], F32, name="o_sb")
-        sorted_back = z[4].rearrange("p (b m) -> p m b", b=16)
-        for c in range(OUT_CHUNKS):
-            roots = slice(c * OUT_ROOTS, (c + 1) * OUT_ROOTS)
-            cols = slice(c * OUT_ROOTS * 16, (c + 1) * OUT_ROOTS * 16)
-            level(4, roots)
+
+        def finish(m0, m1):
+            cols = slice(16 * m0, 16 * m1)
             nc.vector.scalar_tensor_tensor(
-                o_sb[:, cols].rearrange("p (m b) -> p m b", b=16),
-                sorted_back[:, roots, :],
-                R**4,
-                post_sb[:, cols].rearrange("p (m b) -> p m b", b=16),
-                MULT,
-                MULT,
+                grouped(o_sb[:, cols], 4), in_order[4][:, 4 * m0 : 4 * m1, :], R**4, grouped(post_sb[:, cols], 4), MULT, MULT
             )
             nc.sync.dma_start(out[:, cols], o_sb[:, cols])
+
+        odd_level(1, 0, ROOT)
+        even_level(2, 0, ROOT)
+        for step in range(OUT_CHUNKS + 2):
+            for behind in range(3):
+                c = step - behind
+                if 0 <= c < OUT_CHUNKS:
+                    m0, m1 = c * OUT_ROOTS, (c + 1) * OUT_ROOTS
+                    if behind == 0:
+                        odd_level(3, m0, m1)
+                    elif behind == 1:
+                        even_level(4, m0, m1)
+                    else:
+                        finish(m0, m1)

@@ -1,6 +1,7 @@
 import math
 
 import concourse.mybir as mybir
+from concourse.masks import make_identity
 
 F32 = mybir.dt.float32
 U16 = mybir.dt.uint16
@@ -16,9 +17,13 @@ ROOT = S // 16
 F_START = {1: 2048, 2: 1024, 3: 512, 4: 256}
 SIGNS = ((0, 1.0), (1, -1.0))
 
-IN_CHUNKS = 8
+BLOCKS = S // P
+GROUP = 4
+GROUPS = BLOCKS // GROUP
 OUT_CHUNKS = 4
 OUT_ROOTS = ROOT // OUT_CHUNKS
+
+FLOPS = P * (2 * S + N + 4 * (S - ROOT))
 
 
 def grouped(ap, g):
@@ -29,60 +34,83 @@ def across(ap, runs):
     return ap.rearrange("p (r j) -> p j r", r=runs)
 
 
+def coefficient_places(n):
+    return [(0, n >> 4)] + [(n >> k, n >> k) for k in (4, 3, 2, 1)]
+
+
 def tile_waveletlayer_kernel(tc, x, pre, mid, post, offs, out):
     nc = tc.nc
-    pre_row = pre.rearrange("o n -> (o n)")
     mid_row = mid.rearrange("o n -> (o n)")
     post_row = post.rearrange("o n -> (o n)")
 
-    with tc.tile_pool(name="held", bufs=1) as held:
+    with (
+        tc.tile_pool(name="held", bufs=1) as held,
+        tc.tile_pool(name="ring", bufs=3) as ring,
+        tc.psum_pool(name="psum", bufs=2) as psum,
+    ):
         offsets = held.tile([P, N // 16], U16, name="offsets")
         nc.sync.dma_start(offsets[:], offs)
+        pre_rows = held.tile([BLOCKS, P], F32, name="pre_rows")
+        nc.sync.dma_start(pre_rows[:], pre.rearrange("o (b s) -> (o b) s", s=P))
         x_sb = held.tile([P, S], F32, name="x_sb")
-        pre_sb = held.tile([P, S], F32, name="pre_sb")
-        mid_sb = held.tile([P, N], F32, name="mid_sb")
-        post_sb = held.tile([P, S], F32, name="post_sb")
-        for c in range(IN_CHUNKS):
-            cols = slice(c * (S // IN_CHUNKS), (c + 1) * (S // IN_CHUNKS))
+        for g in range(GROUPS):
+            cols = slice(g * GROUP * P, (g + 1) * GROUP * P)
             nc.sync.dma_start(x_sb[:, cols], x[:, cols])
-            nc.scalar.dma_start(pre_sb[:, cols], pre_row[cols].partition_broadcast(P))
+        mid_sb = held.tile([P, N], F32, name="mid_sb")
         nc.sync.dma_start(mid_sb[:], mid_row.partition_broadcast(P))
-        nc.scalar.dma_start(post_sb[:], post_row.partition_broadcast(P))
+        post_sb = held.tile([P, S], F32, name="post_sb")
+        nc.sync.dma_start(post_sb[:], post_row.partition_broadcast(P))
 
-        sums = {0: held.tile([P, S], F32, name="y")}
-        diffs = {}
-        for k in (1, 2, 3):
-            sums[k] = held.tile([P, S >> k], F32, name=f"sum{k}")
-            diffs[k] = held.tile([P, S >> k], F32, name=f"diff{k}")
+        identity = held.tile([P, P], F32, name="identity")
+        make_identity(nc, identity[:])
+        haar = held.tile([P, P], F32, name="haar")
+        sums = held.tile([P, P], F32, name="sum0")
+        nc.vector.tensor_scalar_mul(sums[:], identity[:], R**4)
+        for k in (1, 2, 3, 4):
+            half = P >> k
+            two = grouped(sums[:], 2)
+            sums = held.tile([P, half], F32, name=f"sum{k}")
+            nc.vector.tensor_tensor(sums[:], two[:, :, 0], two[:, :, 1], ADD)
+            diff = held.tile([P, half], F32, name=f"diff{k}")
+            nc.vector.tensor_tensor(diff[:], two[:, :, 0], two[:, :, 1], SUB)
+            nc.vector.tensor_scalar_mul(haar[:, half : 2 * half], diff[:], R ** (k - 4))
+        nc.vector.tensor_copy(haar[:, 0 : P >> 4], sums[:])
+
+        pre_cols_ps = psum.tile([P, GROUP * P], F32, name="flipped_ps")
+        nc.tensor.matmul(pre_cols_ps[:, 0:BLOCKS], pre_rows[:], identity[0:BLOCKS, 0:BLOCKS])
+        pre_cols = held.tile([P, BLOCKS], F32, name="pre_cols")
+        nc.vector.tensor_copy(pre_cols[:], pre_cols_ps[:, 0:BLOCKS])
+
         w = held.tile([P, S], F32, name="w")
+        flipped = {}
 
-        def scale(part, parts):
-            cols = slice(part * (S // parts), (part + 1) * (S // parts))
-            nc.vector.scalar_tensor_tensor(sums[0][:, cols], x_sb[:, cols], R**4, pre_sb[:, cols], MULT, MULT)
+        def flip(g):
+            flipped_ps = psum.tile([P, GROUP * P], F32, name="flipped_ps")
+            flipped[g] = ring.tile([P, GROUP * P], F32, name="flipped")
+            for i in range(GROUP):
+                b = g * GROUP + i
+                nc.tensor.transpose(flipped_ps[:, i * P : (i + 1) * P], x_sb[:, b * P : (b + 1) * P], identity[:])
+            for i in range(GROUP):
+                b = g * GROUP + i
+                nc.scalar.mul(flipped[g][:, i * P : (i + 1) * P], flipped_ps[:, i * P : (i + 1) * P], pre_cols[:, b : b + 1])
 
-        def analyse(k, part, parts):
-            half = (S >> k) // parts
-            two = grouped(sums[k - 1][:, 2 * part * half : 2 * (part + 1) * half], 2)
-            even, odd = two[:, :, 0], two[:, :, 1]
-            here = slice(part * half, (part + 1) * half)
-            in_w = slice((S >> k) + part * half, (S >> k) + (part + 1) * half)
-            if k < 4:
-                nc.vector.tensor_tensor(sums[k][:, here], even, odd, ADD)
-                nc.vector.tensor_tensor(diffs[k][:, here], even, odd, SUB)
-                nc.scalar.mul(w[:, in_w], diffs[k][:, here], R ** (k - 4))
-            else:
-                nc.vector.tensor_tensor(w[:, here], even, odd, ADD)
-                nc.vector.tensor_tensor(w[:, in_w], even, odd, SUB)
+        def multiply(g):
+            product_ps = psum.tile([P, GROUP * P], F32, name="product_ps")
+            for i in range(GROUP):
+                nc.tensor.matmul(product_ps[:, i * P : (i + 1) * P], flipped[g][:, i * P : (i + 1) * P], haar[:])
+            for (in_block, count), (in_w, in_row) in zip(coefficient_places(P), coefficient_places(S)):
+                assert in_row == BLOCKS * count
+                first = in_w + g * GROUP * count
+                nc.vector.tensor_copy(
+                    grouped(w[:, first : first + GROUP * count], count),
+                    grouped(product_ps[:], P)[:, :, in_block : in_block + count],
+                )
 
-        for c in range(IN_CHUNKS + 1):
-            if c < IN_CHUNKS:
-                scale(c, IN_CHUNKS)
-            if c > 0:
-                analyse(2, c - 1, IN_CHUNKS)
-            if c < IN_CHUNKS:
-                analyse(1, c, IN_CHUNKS)
-        analyse(3, 0, 1)
-        analyse(4, 0, 1)
+        flip(0)
+        for g in range(GROUPS):
+            if g + 1 < GROUPS:
+                flip(g + 1)
+            multiply(g)
 
         t = held.tile([P, N], F32, name="t")
         nc.vector.tensor_tensor(t[:], w[:].indirect(offsets[:]), mid_sb[:], MULT)

@@ -8,20 +8,21 @@ U16 = mybir.dt.uint16
 ADD = mybir.AluOpType.add
 SUB = mybir.AluOpType.subtract
 MULT = mybir.AluOpType.mult
+COPY = mybir.ActivationFunctionType.Copy
 
 P = 128
 S = 4096
 N = 2304
 R = math.sqrt(0.5)
 ROOT = S // 16
-F_START = {1: 2048, 2: 1024, 3: 512, 4: 256}
+T_START = {0: 0, 1: 2048, 2: 1024, 3: 512, 4: 256}
 SIGNS = ((0, 1.0), (1, -1.0))
 
-BLOCKS = S // P
 GROUP = 4
-GROUPS = BLOCKS // GROUP
-OUT_CHUNKS = 4
-OUT_ROOTS = ROOT // OUT_CHUNKS
+WIDE = GROUP * P
+GROUPS = S // WIDE
+IN_TENSOR = 4
+OUT_TENSOR = 4
 
 FLOPS = P * (2 * S + N + 4 * (S - ROOT))
 
@@ -34,14 +35,21 @@ def across(ap, runs):
     return ap.rearrange("p (r j) -> p j r", r=runs)
 
 
+def in_runs(ap, runs):
+    return ap.rearrange("p (r j) -> p r j", r=runs)
+
+
 def coefficient_places(n):
     return [(0, n >> 4)] + [(n >> k, n >> k) for k in (4, 3, 2, 1)]
 
 
 def tile_waveletlayer_kernel(tc, x, pre, mid, post, offs, out):
     nc = tc.nc
+    pre_row = pre.rearrange("o n -> (o n)")
     mid_row = mid.rearrange("o n -> (o n)")
     post_row = post.rearrange("o n -> (o n)")
+    in_vector = GROUPS - IN_TENSOR
+    split = IN_TENSOR * WIDE
 
     with (
         tc.tile_pool(name="held", bufs=1) as held,
@@ -50,12 +58,17 @@ def tile_waveletlayer_kernel(tc, x, pre, mid, post, offs, out):
     ):
         offsets = held.tile([P, N // 16], U16, name="offsets")
         nc.sync.dma_start(offsets[:], offs)
-        pre_rows = held.tile([BLOCKS, P], F32, name="pre_rows")
-        nc.sync.dma_start(pre_rows[:], pre.rearrange("o (b s) -> (o b) s", s=P))
+        pre_rows = held.tile([IN_TENSOR * GROUP, P], F32, name="pre_rows")
+        nc.sync.dma_start(pre_rows[:], pre_row[0:split].rearrange("(b s) -> b s", s=P))
         x_sb = held.tile([P, S], F32, name="x_sb")
-        for g in range(GROUPS):
-            cols = slice(g * GROUP * P, (g + 1) * GROUP * P)
-            nc.sync.dma_start(x_sb[:, cols], x[:, cols])
+        pre_sb = held.tile([P, S - split], F32, name="pre_sb")
+        for i in range(max(IN_TENSOR, in_vector)):
+            if i < IN_TENSOR:
+                nc.sync.dma_start(x_sb[:, i * WIDE : (i + 1) * WIDE], x[:, i * WIDE : (i + 1) * WIDE])
+            if i < in_vector:
+                cols = slice(split + i * WIDE, split + (i + 1) * WIDE)
+                nc.sync.dma_start(x_sb[:, cols], x[:, cols])
+                nc.sync.dma_start(pre_sb[:, i * WIDE : (i + 1) * WIDE], pre_row[cols].partition_broadcast(P))
         mid_sb = held.tile([P, N], F32, name="mid_sb")
         nc.sync.dma_start(mid_sb[:], mid_row.partition_broadcast(P))
         post_sb = held.tile([P, S], F32, name="post_sb")
@@ -63,30 +76,30 @@ def tile_waveletlayer_kernel(tc, x, pre, mid, post, offs, out):
 
         identity = held.tile([P, P], F32, name="identity")
         make_identity(nc, identity[:])
+        blocks = IN_TENSOR * GROUP
+        pre_cols_ps = psum.tile([P, WIDE], F32, name="flipped_ps")
+        nc.tensor.matmul(pre_cols_ps[:, 0:blocks], pre_rows[:], identity[0:blocks, 0:blocks])
+        pre_cols = held.tile([P, blocks], F32, name="pre_cols")
+        nc.scalar.activation(pre_cols[:], pre_cols_ps[:, 0:blocks], COPY)
+
         haar = held.tile([P, P], F32, name="haar")
-        sums = held.tile([P, P], F32, name="sum0")
-        nc.vector.tensor_scalar_mul(sums[:], identity[:], R**4)
+        sums = identity
         for k in (1, 2, 3, 4):
             half = P >> k
             two = grouped(sums[:], 2)
-            sums = held.tile([P, half], F32, name=f"sum{k}")
-            nc.vector.tensor_tensor(sums[:], two[:, :, 0], two[:, :, 1], ADD)
-            diff = held.tile([P, half], F32, name=f"diff{k}")
-            nc.vector.tensor_tensor(diff[:], two[:, :, 0], two[:, :, 1], SUB)
-            nc.vector.tensor_scalar_mul(haar[:, half : 2 * half], diff[:], R ** (k - 4))
-        nc.vector.tensor_copy(haar[:, 0 : P >> 4], sums[:])
-
-        pre_cols_ps = psum.tile([P, GROUP * P], F32, name="flipped_ps")
-        nc.tensor.matmul(pre_cols_ps[:, 0:BLOCKS], pre_rows[:], identity[0:BLOCKS, 0:BLOCKS])
-        pre_cols = held.tile([P, BLOCKS], F32, name="pre_cols")
-        nc.vector.tensor_copy(pre_cols[:], pre_cols_ps[:, 0:BLOCKS])
+            sums = held.tile([P, half], F32, name=f"impulse_sum{k}")
+            nc.gpsimd.tensor_tensor(sums[:], two[:, :, 0], two[:, :, 1], ADD)
+            diff = held.tile([P, half], F32, name=f"impulse_diff{k}")
+            nc.gpsimd.tensor_tensor(diff[:], two[:, :, 0], two[:, :, 1], SUB)
+            nc.scalar.mul(haar[:, half : 2 * half], diff[:], R**k)
+        nc.scalar.mul(haar[:, 0 : P >> 4], sums[:], R**4)
 
         w = held.tile([P, S], F32, name="w")
         flipped = {}
 
-        def flip(g):
-            flipped_ps = psum.tile([P, GROUP * P], F32, name="flipped_ps")
-            flipped[g] = ring.tile([P, GROUP * P], F32, name="flipped")
+        def flip_x(g):
+            flipped_ps = psum.tile([P, WIDE], F32, name="flipped_ps")
+            flipped[g] = ring.tile([P, WIDE], F32, name="flipped")
             for i in range(GROUP):
                 b = g * GROUP + i
                 nc.tensor.transpose(flipped_ps[:, i * P : (i + 1) * P], x_sb[:, b * P : (b + 1) * P], identity[:])
@@ -94,26 +107,121 @@ def tile_waveletlayer_kernel(tc, x, pre, mid, post, offs, out):
                 b = g * GROUP + i
                 nc.scalar.mul(flipped[g][:, i * P : (i + 1) * P], flipped_ps[:, i * P : (i + 1) * P], pre_cols[:, b : b + 1])
 
-        def multiply(g):
-            product_ps = psum.tile([P, GROUP * P], F32, name="product_ps")
+        def analyse_on_tensor(g):
+            product_ps = psum.tile([P, WIDE], F32, name="product_ps")
             for i in range(GROUP):
                 nc.tensor.matmul(product_ps[:, i * P : (i + 1) * P], flipped[g][:, i * P : (i + 1) * P], haar[:])
             for (in_block, count), (in_w, in_row) in zip(coefficient_places(P), coefficient_places(S)):
-                assert in_row == BLOCKS * count
                 first = in_w + g * GROUP * count
                 nc.vector.tensor_copy(
                     grouped(w[:, first : first + GROUP * count], count),
                     grouped(product_ps[:], P)[:, :, in_block : in_block + count],
                 )
 
-        flip(0)
-        for g in range(GROUPS):
-            if g + 1 < GROUPS:
-                flip(g + 1)
-            multiply(g)
+        flip_x(0)
+        for g in range(IN_TENSOR):
+            if g + 1 < IN_TENSOR:
+                flip_x(g + 1)
+            analyse_on_tensor(g)
+        haar_flipped_ps = psum.tile([P, WIDE], F32, name="flipped_ps")
+        nc.tensor.transpose(haar_flipped_ps[:, 0:P], haar[:], identity[:])
+        haar_flipped = held.tile([P, P], F32, name="haar_flipped")
+        nc.scalar.activation(haar_flipped[:], haar_flipped_ps[:, 0:P], COPY)
+
+        y_runs = held.tile([P, S - split], F32, name="y_runs")
+        sum1 = held.tile([P, (S - split) >> 1], F32, name="sum1")
+        diff1 = held.tile([P, (S - split) >> 1], F32, name="diff1")
+        diff2 = held.tile([P, (S - split) >> 2], F32, name="diff2")
+        sum2_runs = held.tile([P, (S - split) >> 2], F32, name="sum2_runs")
+        sum3 = held.tile([P, (S - split) >> 3], F32, name="sum3")
+        diff3 = held.tile([P, (S - split) >> 3], F32, name="diff3")
+
+        def odd_analysis(k, four_runs, two_runs, diff_runs, first):
+            n = four_runs.shape[1]
+            pairs = four_runs.rearrange("p (h e i) -> p e h i", h=2, e=2)
+            nc.vector.tensor_tensor(in_runs(two_runs, 2), pairs[:, 0], pairs[:, 1], ADD)
+            nc.vector.tensor_tensor(in_runs(diff_runs, 2), pairs[:, 0], pairs[:, 1], SUB)
+            nc.scalar.mul(grouped(w[:, first : first + n // 2], 2), across(diff_runs, 2), R ** (k - 4))
+
+        def scale(v):
+            cols = slice(v * WIDE, (v + 1) * WIDE)
+            nc.vector.scalar_tensor_tensor(
+                across(y_runs[:, cols], 4),
+                grouped(x_sb[:, split + v * WIDE : split + (v + 1) * WIDE], 4),
+                R**4,
+                grouped(pre_sb[:, cols], 4),
+                MULT,
+                MULT,
+            )
+
+        def first_level(v):
+            half = slice(v * WIDE // 2, (v + 1) * WIDE // 2)
+            odd_analysis(1, y_runs[:, v * WIDE : (v + 1) * WIDE], sum1[:, half], diff1[:, half], (S + split + v * WIDE) >> 1)
+
+        def second_level(v):
+            n = WIDE // 4
+            even = sum1[:, 2 * v * n : (2 * v + 1) * n]
+            odd = sum1[:, (2 * v + 1) * n : (2 * v + 2) * n]
+            nc.vector.tensor_tensor(
+                across(sum2_runs[:], 4)[:, v * n // 4 : (v + 1) * n // 4, :], grouped(even, 4), grouped(odd, 4), ADD
+            )
+            nc.vector.tensor_tensor(diff2[:, v * n : (v + 1) * n], even, odd, SUB)
+            first = (S + split + v * WIDE) >> 2
+            nc.scalar.mul(w[:, first : first + n], diff2[:, v * n : (v + 1) * n], R ** (2 - 4))
+
+        for v in range(in_vector + 1):
+            if v < in_vector:
+                scale(v)
+            if v > 0:
+                second_level(v - 1)
+            if v < in_vector:
+                first_level(v)
+        odd_analysis(3, sum2_runs[:], sum3[:], diff3[:], (S + split) >> 3)
+        n = (S - split) >> 4
+        nc.vector.tensor_tensor(w[:, split >> 4 : S >> 4], sum3[:, 0:n], sum3[:, n : 2 * n], ADD)
+        nc.vector.tensor_tensor(w[:, (S + split) >> 4 : S >> 3], sum3[:, 0:n], sum3[:, n : 2 * n], SUB)
 
         t = held.tile([P, N], F32, name="t")
-        nc.vector.tensor_tensor(t[:], w[:].indirect(offsets[:]), mid_sb[:], MULT)
+        blocks = OUT_TENSOR * GROUP
+        early = [(T_START[k], T_START[k] + blocks * count) for k, count in ((0, P >> 4), (4, P >> 1), (1, P >> 4))]
+        assert early[1][0] <= T_START[3] and T_START[3] + blocks * (P >> 2) <= early[1][1]
+        assert early[1][0] <= T_START[2] and T_START[2] + blocks * (P >> 3) <= early[1][1]
+        late = [(early[0][1], early[1][0]), (early[1][1], early[2][0]), (early[2][1], N)]
+        for first, last in early + late:
+            nc.vector.tensor_tensor(
+                t[:, first:last], w[:].indirect(offsets[:, first // 16 : last // 16]), mid_sb[:, first:last], MULT
+            )
+
+        o_sb = held.tile([P, S], F32, name="o_sb")
+
+        def flip_t(g):
+            packed = ring.tile([P, WIDE], F32, name="packed")
+            for k, (in_block, count) in enumerate(coefficient_places(P)):
+                first = T_START[k] + g * GROUP * count
+                nc.scalar.activation(
+                    grouped(packed[:], P)[:, :, in_block : in_block + count],
+                    grouped(t[:, first : first + GROUP * count], count),
+                    COPY,
+                )
+            flipped_ps = psum.tile([P, WIDE], F32, name="flipped_ps")
+            for i in range(GROUP):
+                nc.tensor.transpose(flipped_ps[:, i * P : (i + 1) * P], packed[:, i * P : (i + 1) * P], identity[:])
+            flipped[g] = ring.tile([P, WIDE], F32, name="flipped")
+            nc.scalar.activation(flipped[g][:], flipped_ps[:], COPY)
+
+        def synthesise_on_tensor(g):
+            product_ps = psum.tile([P, WIDE], F32, name="product_ps")
+            for i in range(GROUP):
+                nc.tensor.matmul(product_ps[:, i * P : (i + 1) * P], flipped[g][:, i * P : (i + 1) * P], haar_flipped[:])
+            cols = slice(g * WIDE, (g + 1) * WIDE)
+            nc.vector.tensor_tensor(o_sb[:, cols], product_ps[:], post_sb[:, cols], MULT)
+            nc.sync.dma_start(out[:, cols], o_sb[:, cols])
+
+        flip_t(0)
+        for g in range(OUT_TENSOR):
+            if g + 1 < OUT_TENSOR:
+                flip_t(g + 1)
+            synthesise_on_tensor(g)
 
         halves = {k: held.tile([P, ROOT << k], F32, name=f"halves{k}") for k in (1, 3)}
         quarters = {k: held.tile([P, ROOT << k], F32, name=f"quarters{k}") for k in (2, 4)}
@@ -122,7 +230,7 @@ def tile_waveletlayer_kernel(tc, x, pre, mid, post, offs, out):
         def odd_level(k, m0, m1):
             g = 1 << (k - 1)
             n = ROOT * g
-            f_k = t[:, F_START[k] + g * m0 : F_START[k] + g * m1]
+            f_k = t[:, T_START[k] + g * m0 : T_START[k] + g * m1]
             for s, sign in SIGNS:
                 nc.vector.scalar_tensor_tensor(
                     grouped(halves[k][:, s * n + g * m0 : s * n + g * m1], g),
@@ -135,7 +243,7 @@ def tile_waveletlayer_kernel(tc, x, pre, mid, post, offs, out):
 
         def even_level(k, m0, m1):
             g = 1 << (k - 2)
-            f_k = t[:, F_START[k] + 2 * g * m0 : F_START[k] + 2 * g * m1]
+            f_k = t[:, T_START[k] + 2 * g * m0 : T_START[k] + 2 * g * m1]
             by_sign = quarters[k].rearrange("p (s1 s2 j) -> p s2 j s1", s1=2, s2=2)
             for s, sign in SIGNS:
                 nc.vector.scalar_tensor_tensor(
@@ -147,8 +255,6 @@ def tile_waveletlayer_kernel(tc, x, pre, mid, post, offs, out):
                     ADD,
                 )
 
-        o_sb = held.tile([P, S], F32, name="o_sb")
-
         def finish(m0, m1):
             cols = slice(16 * m0, 16 * m1)
             nc.vector.scalar_tensor_tensor(
@@ -156,16 +262,16 @@ def tile_waveletlayer_kernel(tc, x, pre, mid, post, offs, out):
             )
             nc.sync.dma_start(out[:, cols], o_sb[:, cols])
 
-        odd_level(1, 0, ROOT)
-        even_level(2, 0, ROOT)
-        for step in range(OUT_CHUNKS + 2):
+        roots = WIDE // 16
+        odd_level(1, OUT_TENSOR * roots, ROOT)
+        even_level(2, OUT_TENSOR * roots, ROOT)
+        for step in range(OUT_TENSOR, GROUPS + 2):
             for behind in range(3):
-                c = step - behind
-                if 0 <= c < OUT_CHUNKS:
-                    m0, m1 = c * OUT_ROOTS, (c + 1) * OUT_ROOTS
+                g = step - behind
+                if OUT_TENSOR <= g < GROUPS:
                     if behind == 0:
-                        odd_level(3, m0, m1)
+                        odd_level(3, g * roots, (g + 1) * roots)
                     elif behind == 1:
-                        even_level(4, m0, m1)
+                        even_level(4, g * roots, (g + 1) * roots)
                     else:
-                        finish(m0, m1)
+                        finish(g * roots, (g + 1) * roots)

@@ -35,10 +35,6 @@ def across(ap, runs):
     return ap.rearrange("p (r j) -> p j r", r=runs)
 
 
-def in_runs(ap, runs):
-    return ap.rearrange("p (r j) -> p r j", r=runs)
-
-
 def coefficient_places(n):
     return [(0, n >> 4)] + [(n >> k, n >> k) for k in (4, 3, 2, 1)]
 
@@ -128,46 +124,39 @@ def tile_waveletlayer_kernel(tc, x, pre, mid, post, offs, out):
         haar_flipped = held.tile([P, P], F32, name="haar_flipped")
         nc.scalar.activation(haar_flipped[:], haar_flipped_ps[:, 0:P], COPY)
 
-        y_runs = held.tile([P, S - split], F32, name="y_runs")
-        sum1 = held.tile([P, (S - split) >> 1], F32, name="sum1")
-        diff1 = held.tile([P, (S - split) >> 1], F32, name="diff1")
-        diff2 = held.tile([P, (S - split) >> 2], F32, name="diff2")
-        sum2_runs = held.tile([P, (S - split) >> 2], F32, name="sum2_runs")
-        sum3 = held.tile([P, (S - split) >> 3], F32, name="sum3")
-        diff3 = held.tile([P, (S - split) >> 3], F32, name="diff3")
-
-        def odd_analysis(k, four_runs, two_runs, diff_runs, first):
-            n = four_runs.shape[1]
-            pairs = four_runs.rearrange("p (h e i) -> p e h i", h=2, e=2)
-            nc.vector.tensor_tensor(in_runs(two_runs, 2), pairs[:, 0], pairs[:, 1], ADD)
-            nc.vector.tensor_tensor(in_runs(diff_runs, 2), pairs[:, 0], pairs[:, 1], SUB)
-            nc.scalar.mul(grouped(w[:, first : first + n // 2], 2), across(diff_runs, 2), R ** (k - 4))
+        sums = {k: held.tile([P, (S - split) >> k], F32, name=f"sum{k}") for k in (0, 1, 2, 3)}
+        diffs = {k: held.tile([P, (S - split) >> k], F32, name=f"diff{k}") for k in (1, 2, 3)}
 
         def scale(v):
             cols = slice(v * WIDE, (v + 1) * WIDE)
             nc.vector.scalar_tensor_tensor(
-                across(y_runs[:, cols], 4),
-                grouped(x_sb[:, split + v * WIDE : split + (v + 1) * WIDE], 4),
+                across(sums[0][:, cols], 2),
+                grouped(x_sb[:, split + v * WIDE : split + (v + 1) * WIDE], 2),
                 R**4,
-                grouped(pre_sb[:, cols], 4),
+                grouped(pre_sb[:, cols], 2),
                 MULT,
                 MULT,
             )
+
+        def halve(k, two_runs, sum_to, first):
+            n = two_runs.shape[1] // 2
+            even, odd = two_runs[:, 0:n], two_runs[:, n : 2 * n]
+            d_k = slice((S >> k) + first, (S >> k) + first + n)
+            if k < 4:
+                nc.vector.tensor_tensor(sum_to, grouped(even, 2), grouped(odd, 2), ADD)
+                here = slice(first - (split >> k), first - (split >> k) + n)
+                nc.vector.tensor_tensor(diffs[k][:, here], even, odd, SUB)
+                nc.scalar.mul(w[:, d_k], diffs[k][:, here], R ** (k - 4))
+            else:
+                nc.vector.tensor_tensor(w[:, first : first + n], even, odd, ADD)
+                nc.vector.tensor_tensor(w[:, d_k], even, odd, SUB)
 
         def first_level(v):
-            half = slice(v * WIDE // 2, (v + 1) * WIDE // 2)
-            odd_analysis(1, y_runs[:, v * WIDE : (v + 1) * WIDE], sum1[:, half], diff1[:, half], (S + split + v * WIDE) >> 1)
+            halve(1, sums[0][:, v * WIDE : (v + 1) * WIDE], across(sums[1][:, v * WIDE // 2 : (v + 1) * WIDE // 2], 2), (split + v * WIDE) >> 1)
 
         def second_level(v):
-            n = WIDE // 4
-            even = sum1[:, 2 * v * n : (2 * v + 1) * n]
-            odd = sum1[:, (2 * v + 1) * n : (2 * v + 2) * n]
-            nc.vector.tensor_tensor(
-                across(sum2_runs[:], 4)[:, v * n // 4 : (v + 1) * n // 4, :], grouped(even, 4), grouped(odd, 4), ADD
-            )
-            nc.vector.tensor_tensor(diff2[:, v * n : (v + 1) * n], even, odd, SUB)
-            first = (S + split + v * WIDE) >> 2
-            nc.scalar.mul(w[:, first : first + n], diff2[:, v * n : (v + 1) * n], R ** (2 - 4))
+            rows = slice(v * WIDE // 8, (v + 1) * WIDE // 8)
+            halve(2, sums[1][:, v * WIDE // 2 : (v + 1) * WIDE // 2], across(sums[2][:], 2)[:, rows, :], (split + v * WIDE) >> 2)
 
         for v in range(in_vector + 1):
             if v < in_vector:
@@ -176,10 +165,8 @@ def tile_waveletlayer_kernel(tc, x, pre, mid, post, offs, out):
                 second_level(v - 1)
             if v < in_vector:
                 first_level(v)
-        odd_analysis(3, sum2_runs[:], sum3[:], diff3[:], (S + split) >> 3)
-        n = (S - split) >> 4
-        nc.vector.tensor_tensor(w[:, split >> 4 : S >> 4], sum3[:, 0:n], sum3[:, n : 2 * n], ADD)
-        nc.vector.tensor_tensor(w[:, (S + split) >> 4 : S >> 3], sum3[:, 0:n], sum3[:, n : 2 * n], SUB)
+        halve(3, sums[2][:], across(sums[3][:], 2), split >> 3)
+        halve(4, sums[3][:], None, split >> 4)
 
         t = held.tile([P, N], F32, name="t")
         blocks = OUT_TENSOR * GROUP
@@ -223,55 +210,41 @@ def tile_waveletlayer_kernel(tc, x, pre, mid, post, offs, out):
                 flip_t(g + 1)
             synthesise_on_tensor(g)
 
-        halves = {k: held.tile([P, ROOT << k], F32, name=f"halves{k}") for k in (1, 3)}
-        quarters = {k: held.tile([P, ROOT << k], F32, name=f"quarters{k}") for k in (2, 4)}
-        in_order = {0: grouped(t[:, 0:ROOT], 1), 2: across(quarters[2], 4), 4: across(quarters[4], 4)}
+        halves = {k: held.tile([P, ROOT << k], F32, name=f"halves{k}") for k in (1, 2, 3, 4)}
 
-        def odd_level(k, m0, m1):
+        def double(k, m0, m1):
             g = 1 << (k - 1)
             n = ROOT * g
             f_k = t[:, T_START[k] + g * m0 : T_START[k] + g * m1]
             for s, sign in SIGNS:
-                nc.vector.scalar_tensor_tensor(
-                    grouped(halves[k][:, s * n + g * m0 : s * n + g * m1], g),
-                    grouped(f_k, g),
-                    sign * R ** (1 - k),
-                    in_order[k - 1][:, m0:m1, :],
-                    MULT,
-                    ADD,
-                )
-
-        def even_level(k, m0, m1):
-            g = 1 << (k - 2)
-            f_k = t[:, T_START[k] + 2 * g * m0 : T_START[k] + 2 * g * m1]
-            by_sign = quarters[k].rearrange("p (s1 s2 j) -> p s2 j s1", s1=2, s2=2)
-            for s, sign in SIGNS:
-                nc.vector.scalar_tensor_tensor(
-                    by_sign[:, s, g * m0 : g * m1, :],
-                    grouped(f_k, 2),
-                    sign * R ** (1 - k),
-                    across(halves[k - 1], 2)[:, g * m0 : g * m1, :],
-                    MULT,
-                    ADD,
-                )
+                run = halves[k][:, s * n + g * m0 : s * n + g * m1]
+                if k == 1:
+                    nc.vector.scalar_tensor_tensor(run, f_k, sign, t[:, m0:m1], MULT, ADD)
+                else:
+                    nc.vector.scalar_tensor_tensor(
+                        grouped(run, 2),
+                        grouped(f_k, 2),
+                        sign * R ** (1 - k),
+                        across(halves[k - 1], 2)[:, g * m0 // 2 : g * m1 // 2, :],
+                        MULT,
+                        ADD,
+                    )
 
         def finish(m0, m1):
             cols = slice(16 * m0, 16 * m1)
             nc.vector.scalar_tensor_tensor(
-                grouped(o_sb[:, cols], 4), in_order[4][:, 4 * m0 : 4 * m1, :], R**4, grouped(post_sb[:, cols], 4), MULT, MULT
+                grouped(o_sb[:, cols], 2), across(halves[4], 2)[:, 8 * m0 : 8 * m1, :], R**4, grouped(post_sb[:, cols], 2), MULT, MULT
             )
             nc.sync.dma_start(out[:, cols], o_sb[:, cols])
 
         roots = WIDE // 16
-        odd_level(1, OUT_TENSOR * roots, ROOT)
-        even_level(2, OUT_TENSOR * roots, ROOT)
+        double(1, OUT_TENSOR * roots, ROOT)
+        double(2, OUT_TENSOR * roots, ROOT)
         for step in range(OUT_TENSOR, GROUPS + 2):
             for behind in range(3):
                 g = step - behind
                 if OUT_TENSOR <= g < GROUPS:
-                    if behind == 0:
-                        odd_level(3, g * roots, (g + 1) * roots)
-                    elif behind == 1:
-                        even_level(4, g * roots, (g + 1) * roots)
+                    if behind < 2:
+                        double(3 + behind, g * roots, (g + 1) * roots)
                     else:
                         finish(g * roots, (g + 1) * roots)

@@ -54,25 +54,21 @@ def tile_waveletlayer_kernel(tc, x, pre, mid, post, offs, out):
     ):
         offsets = held.tile([P, N // 16], U16, name="offsets")
         nc.sync.dma_start(offsets[:], offs)
-        pre_rows = held.tile([IN_TENSOR * GROUP, P], F32, name="pre_rows")
-        nc.sync.dma_start(pre_rows[:], pre_row[0:split].rearrange("(b s) -> b s", s=P))
-        x_sb = held.tile([P, S], F32, name="x_sb")
-        pre_sb = held.tile([P, S - split], F32, name="pre_sb")
-        for i in range(max(IN_TENSOR, in_vector)):
-            if i < IN_TENSOR:
-                nc.sync.dma_start(x_sb[:, i * WIDE : (i + 1) * WIDE], x[:, i * WIDE : (i + 1) * WIDE])
-            if i < in_vector:
-                cols = slice(split + i * WIDE, split + (i + 1) * WIDE)
-                nc.sync.dma_start(x_sb[:, cols], x[:, cols])
-                nc.sync.dma_start(pre_sb[:, i * WIDE : (i + 1) * WIDE], pre_row[cols].partition_broadcast(P))
+        pre_rows = held.tile([S // P, P], F32, name="pre_rows")
+        nc.sync.dma_start(pre_rows[:], pre_row.rearrange("(b s) -> b s", s=P))
         mid_sb = held.tile([P, N], F32, name="mid_sb")
-        nc.sync.dma_start(mid_sb[:], mid_row.partition_broadcast(P))
+        nc.scalar.dma_start(mid_sb[:], mid_row.partition_broadcast(P))
         post_sb = held.tile([P, S], F32, name="post_sb")
-        nc.sync.dma_start(post_sb[:], post_row.partition_broadcast(P))
+        nc.scalar.dma_start(post_sb[:, 0 : S // 2], post_row[0 : S // 2].partition_broadcast(P))
+        x_sb = held.tile([P, S], F32, name="x_sb")
+        for i in range(max(IN_TENSOR, in_vector)):
+            for g in [i] * (i < IN_TENSOR) + [IN_TENSOR + i] * (i < in_vector):
+                nc.sync.dma_start(x_sb[:, g * WIDE : (g + 1) * WIDE], x[:, g * WIDE : (g + 1) * WIDE])
+        nc.sync.dma_start(post_sb[:, S // 2 : S], post_row[S // 2 : S].partition_broadcast(P))
 
         identity = held.tile([P, P], F32, name="identity")
         make_identity(nc, identity[:])
-        blocks = IN_TENSOR * GROUP
+        blocks = S // P
         pre_cols_ps = psum.tile([P, WIDE], F32, name="flipped_ps")
         nc.tensor.matmul(pre_cols_ps[:, 0:blocks], pre_rows[:], identity[0:blocks, 0:blocks])
         pre_cols = held.tile([P, blocks], F32, name="pre_cols")
@@ -128,12 +124,15 @@ def tile_waveletlayer_kernel(tc, x, pre, mid, post, offs, out):
         diffs = {k: held.tile([P, (S - split) >> k], F32, name=f"diff{k}") for k in (1, 2, 3)}
 
         def scale(v):
-            cols = slice(v * WIDE, (v + 1) * WIDE)
+            pre_ps = psum.tile([P, WIDE], F32, name="pre_ps")
+            for i in range(GROUP):
+                b = (IN_TENSOR + v) * GROUP + i
+                nc.tensor.transpose(pre_ps[:, i * P : (i + 1) * P], pre_cols[:, b : b + 1].to_broadcast([P, P]), identity[:])
             nc.vector.scalar_tensor_tensor(
-                across(sums[0][:, cols], 2),
+                across(sums[0][:, v * WIDE : (v + 1) * WIDE], 2),
                 grouped(x_sb[:, split + v * WIDE : split + (v + 1) * WIDE], 2),
                 R**4,
-                grouped(pre_sb[:, cols], 2),
+                grouped(pre_ps[:], 2),
                 MULT,
                 MULT,
             )

@@ -21,8 +21,8 @@ SIGNS = ((0, 1.0), (1, -1.0))
 GROUP = 4
 WIDE = GROUP * P
 GROUPS = S // WIDE
-IN_TENSOR = 4
-OUT_TENSOR = 4
+IN_TENSOR = 6
+OUT_TENSOR = 6
 
 FLOPS = P * (2 * S + N + 4 * (S - ROOT))
 
@@ -54,21 +54,25 @@ def tile_waveletlayer_kernel(tc, x, pre, mid, post, offs, out):
     ):
         offsets = held.tile([P, N // 16], U16, name="offsets")
         nc.sync.dma_start(offsets[:], offs)
-        pre_rows = held.tile([S // P, P], F32, name="pre_rows")
-        nc.sync.dma_start(pre_rows[:], pre_row.rearrange("(b s) -> b s", s=P))
-        mid_sb = held.tile([P, N], F32, name="mid_sb")
-        nc.scalar.dma_start(mid_sb[:], mid_row.partition_broadcast(P))
-        post_sb = held.tile([P, S], F32, name="post_sb")
-        nc.scalar.dma_start(post_sb[:, 0 : S // 2], post_row[0 : S // 2].partition_broadcast(P))
+        pre_rows = held.tile([IN_TENSOR * GROUP, P], F32, name="pre_rows")
+        nc.sync.dma_start(pre_rows[:], pre_row[0:split].rearrange("(b s) -> b s", s=P))
         x_sb = held.tile([P, S], F32, name="x_sb")
+        pre_sb = held.tile([P, S - split], F32, name="pre_sb")
         for i in range(max(IN_TENSOR, in_vector)):
-            for g in [i] * (i < IN_TENSOR) + [IN_TENSOR + i] * (i < in_vector):
-                nc.sync.dma_start(x_sb[:, g * WIDE : (g + 1) * WIDE], x[:, g * WIDE : (g + 1) * WIDE])
-        nc.sync.dma_start(post_sb[:, S // 2 : S], post_row[S // 2 : S].partition_broadcast(P))
+            if i < IN_TENSOR:
+                nc.sync.dma_start(x_sb[:, i * WIDE : (i + 1) * WIDE], x[:, i * WIDE : (i + 1) * WIDE])
+            if i < in_vector:
+                cols = slice(split + i * WIDE, split + (i + 1) * WIDE)
+                nc.sync.dma_start(x_sb[:, cols], x[:, cols])
+                nc.sync.dma_start(pre_sb[:, i * WIDE : (i + 1) * WIDE], pre_row[cols].partition_broadcast(P))
+        mid_sb = held.tile([P, N], F32, name="mid_sb")
+        nc.sync.dma_start(mid_sb[:], mid_row.partition_broadcast(P))
+        post_sb = held.tile([P, S], F32, name="post_sb")
+        nc.sync.dma_start(post_sb[:], post_row.partition_broadcast(P))
 
         identity = held.tile([P, P], F32, name="identity")
         make_identity(nc, identity[:])
-        blocks = S // P
+        blocks = IN_TENSOR * GROUP
         pre_cols_ps = psum.tile([P, WIDE], F32, name="flipped_ps")
         nc.tensor.matmul(pre_cols_ps[:, 0:blocks], pre_rows[:], identity[0:blocks, 0:blocks])
         pre_cols = held.tile([P, blocks], F32, name="pre_cols")
@@ -124,15 +128,12 @@ def tile_waveletlayer_kernel(tc, x, pre, mid, post, offs, out):
         diffs = {k: held.tile([P, (S - split) >> k], F32, name=f"diff{k}") for k in (1, 2, 3)}
 
         def scale(v):
-            pre_ps = psum.tile([P, WIDE], F32, name="pre_ps")
-            for i in range(GROUP):
-                b = (IN_TENSOR + v) * GROUP + i
-                nc.tensor.transpose(pre_ps[:, i * P : (i + 1) * P], pre_cols[:, b : b + 1].to_broadcast([P, P]), identity[:])
+            cols = slice(v * WIDE, (v + 1) * WIDE)
             nc.vector.scalar_tensor_tensor(
-                across(sums[0][:, v * WIDE : (v + 1) * WIDE], 2),
+                across(sums[0][:, cols], 2),
                 grouped(x_sb[:, split + v * WIDE : split + (v + 1) * WIDE], 2),
                 R**4,
-                grouped(pre_ps[:], 2),
+                grouped(pre_sb[:, cols], 2),
                 MULT,
                 MULT,
             )
@@ -168,12 +169,8 @@ def tile_waveletlayer_kernel(tc, x, pre, mid, post, offs, out):
         halve(4, sums[3][:], None, split >> 4)
 
         t = held.tile([P, N], F32, name="t")
-        blocks = OUT_TENSOR * GROUP
-        early = [(T_START[k], T_START[k] + blocks * count) for k, count in ((0, P >> 4), (4, P >> 1), (1, P >> 4))]
-        assert early[1][0] <= T_START[3] and T_START[3] + blocks * (P >> 2) <= early[1][1]
-        assert early[1][0] <= T_START[2] and T_START[2] + blocks * (P >> 3) <= early[1][1]
-        late = [(early[0][1], early[1][0]), (early[1][1], early[2][0]), (early[2][1], N)]
-        for first, last in early + late:
+        pieces = [(0, ROOT), (T_START[1], N)] + [(first, first + WIDE // 2) for first in range(T_START[4], T_START[1], WIDE // 2)]
+        for first, last in pieces:
             nc.vector.tensor_tensor(
                 t[:, first:last], w[:].indirect(offsets[:, first // 16 : last // 16]), mid_sb[:, first:last], MULT
             )

@@ -21,8 +21,8 @@ SIGNS = ((0, 1.0), (1, -1.0))
 GROUP = 4
 WIDE = GROUP * P
 GROUPS = S // WIDE
-IN_TENSOR = 6
-OUT_TENSOR = 6
+IN_TENSOR = GROUPS // 2
+OUT_TENSOR = GROUPS // 2
 
 FLOPS = P * (2 * S + N + 4 * (S - ROOT))
 
@@ -51,32 +51,48 @@ def tile_waveletlayer_kernel(tc, x, pre, mid, post, offs, out):
         tc.tile_pool(name="held", bufs=1) as held,
         tc.tile_pool(name="ring", bufs=3) as ring,
         tc.psum_pool(name="psum", bufs=2) as psum,
+        tc.psum_pool(name="spreads", bufs=GROUPS - OUT_TENSOR) as spreads,
     ):
         offsets = held.tile([P, N // 16], U16, name="offsets")
         nc.sync.dma_start(offsets[:], offs)
-        pre_rows = held.tile([IN_TENSOR * GROUP, P], F32, name="pre_rows")
-        nc.sync.dma_start(pre_rows[:], pre_row[0:split].rearrange("(b s) -> b s", s=P))
+        pre_rows = held.tile([S // P, P], F32, name="pre_rows")
+        nc.sync.dma_start(pre_rows[:], pre_row.rearrange("(b s) -> b s", s=P))
+        out_split = OUT_TENSOR * WIDE
+        post_rows = held.tile([(S - out_split) // P, P], F32, name="post_rows")
+        nc.sync.dma_start(post_rows[:], post_row[out_split:S].rearrange("(b s) -> b s", s=P))
         x_sb = held.tile([P, S], F32, name="x_sb")
-        pre_sb = held.tile([P, S - split], F32, name="pre_sb")
         for i in range(max(IN_TENSOR, in_vector)):
             if i < IN_TENSOR:
                 nc.sync.dma_start(x_sb[:, i * WIDE : (i + 1) * WIDE], x[:, i * WIDE : (i + 1) * WIDE])
             if i < in_vector:
-                cols = slice(split + i * WIDE, split + (i + 1) * WIDE)
-                nc.sync.dma_start(x_sb[:, cols], x[:, cols])
-                nc.sync.dma_start(pre_sb[:, i * WIDE : (i + 1) * WIDE], pre_row[cols].partition_broadcast(P))
+                nc.sync.dma_start(x_sb[:, split + i * WIDE : split + (i + 1) * WIDE], x[:, split + i * WIDE : split + (i + 1) * WIDE])
         mid_sb = held.tile([P, N], F32, name="mid_sb")
-        nc.sync.dma_start(mid_sb[:], mid_row.partition_broadcast(P))
-        post_sb = held.tile([P, S], F32, name="post_sb")
-        nc.sync.dma_start(post_sb[:], post_row.partition_broadcast(P))
+        mid_cut = T_START[4] + OUT_TENSOR * WIDE // 2
+        for cols in (slice(0, mid_cut), slice(mid_cut, N)):
+            nc.sync.dma_start(mid_sb[:, cols], mid_row[cols].partition_broadcast(P))
+        post_sb = held.tile([P, out_split], F32, name="post_sb")
+        for cols in (slice(0, out_split // 2), slice(out_split // 2, out_split)):
+            nc.sync.dma_start(post_sb[:, cols], post_row[cols].partition_broadcast(P))
 
         identity = held.tile([P, P], F32, name="identity")
         make_identity(nc, identity[:])
-        blocks = IN_TENSOR * GROUP
-        pre_cols_ps = psum.tile([P, WIDE], F32, name="flipped_ps")
-        nc.tensor.matmul(pre_cols_ps[:, 0:blocks], pre_rows[:], identity[0:blocks, 0:blocks])
-        pre_cols = held.tile([P, blocks], F32, name="pre_cols")
-        nc.scalar.activation(pre_cols[:], pre_cols_ps[:, 0:blocks], COPY)
+
+        def blocks_to_columns(rows, name):
+            blocks = rows.shape[0]
+            columns_ps = psum.tile([P, WIDE], F32, name="flipped_ps")
+            nc.tensor.matmul(columns_ps[:, 0:blocks], rows, identity[0:blocks, 0:blocks])
+            columns = held.tile([P, blocks], F32, name=name)
+            nc.scalar.activation(columns[:], columns_ps[:, 0:blocks], COPY)
+            return columns
+
+        def spread(columns, first):
+            spread_ps = spreads.tile([P, WIDE], F32, name="spread_ps")
+            for i in range(GROUP):
+                one = columns[:, first + i : first + i + 1]
+                nc.tensor.transpose(spread_ps[:, i * P : (i + 1) * P], one.to_broadcast([P, P]), identity[:])
+            return spread_ps
+
+        pre_cols = blocks_to_columns(pre_rows[:], "pre_cols")
 
         haar = held.tile([P, P], F32, name="haar")
         sums = identity
@@ -107,33 +123,24 @@ def tile_waveletlayer_kernel(tc, x, pre, mid, post, offs, out):
             product_ps = psum.tile([P, WIDE], F32, name="product_ps")
             for i in range(GROUP):
                 nc.tensor.matmul(product_ps[:, i * P : (i + 1) * P], flipped[g][:, i * P : (i + 1) * P], haar[:])
-            for (in_block, count), (in_w, in_row) in zip(coefficient_places(P), coefficient_places(S)):
-                first = in_w + g * GROUP * count
-                nc.vector.tensor_copy(
+            for (in_block, count), in_w in zip(coefficient_places(P), coefficient_places(S)):
+                first = in_w[0] + g * GROUP * count
+                nc.scalar.activation(
                     grouped(w[:, first : first + GROUP * count], count),
                     grouped(product_ps[:], P)[:, :, in_block : in_block + count],
+                    COPY,
                 )
-
-        flip_x(0)
-        for g in range(IN_TENSOR):
-            if g + 1 < IN_TENSOR:
-                flip_x(g + 1)
-            analyse_on_tensor(g)
-        haar_flipped_ps = psum.tile([P, WIDE], F32, name="flipped_ps")
-        nc.tensor.transpose(haar_flipped_ps[:, 0:P], haar[:], identity[:])
-        haar_flipped = held.tile([P, P], F32, name="haar_flipped")
-        nc.scalar.activation(haar_flipped[:], haar_flipped_ps[:, 0:P], COPY)
 
         sums = {k: held.tile([P, (S - split) >> k], F32, name=f"sum{k}") for k in (0, 1, 2, 3)}
         diffs = {k: held.tile([P, (S - split) >> k], F32, name=f"diff{k}") for k in (1, 2, 3)}
 
         def scale(v):
-            cols = slice(v * WIDE, (v + 1) * WIDE)
+            pre_ps = spread(pre_cols, (IN_TENSOR + v) * GROUP)
             nc.vector.scalar_tensor_tensor(
-                across(sums[0][:, cols], 2),
+                across(sums[0][:, v * WIDE : (v + 1) * WIDE], 2),
                 grouped(x_sb[:, split + v * WIDE : split + (v + 1) * WIDE], 2),
                 R**4,
-                grouped(pre_sb[:, cols], 2),
+                grouped(pre_ps[:], 2),
                 MULT,
                 MULT,
             )
@@ -158,19 +165,35 @@ def tile_waveletlayer_kernel(tc, x, pre, mid, post, offs, out):
             rows = slice(v * WIDE // 8, (v + 1) * WIDE // 8)
             halve(2, sums[1][:, v * WIDE // 2 : (v + 1) * WIDE // 2], across(sums[2][:], 2)[:, rows, :], (split + v * WIDE) >> 2)
 
-        for v in range(in_vector + 1):
-            if v < in_vector:
-                scale(v)
-            if v > 0:
-                second_level(v - 1)
-            if v < in_vector:
-                first_level(v)
+        for i in range(max(IN_TENSOR, in_vector) + 1):
+            if i < in_vector:
+                scale(i)
+            if i < IN_TENSOR:
+                flip_x(i)
+            if 0 < i <= IN_TENSOR:
+                analyse_on_tensor(i - 1)
+            if 0 < i <= in_vector:
+                second_level(i - 1)
+            if i < in_vector:
+                first_level(i)
         halve(3, sums[2][:], across(sums[3][:], 2), split >> 3)
         halve(4, sums[3][:], None, split >> 4)
 
+        haar_flipped_ps = psum.tile([P, WIDE], F32, name="flipped_ps")
+        nc.tensor.transpose(haar_flipped_ps[:, 0:P], haar[:], identity[:])
+        haar_flipped = held.tile([P, P], F32, name="haar_flipped")
+        nc.scalar.activation(haar_flipped[:], haar_flipped_ps[:, 0:P], COPY)
+
+        post_cols = blocks_to_columns(post_rows[:], "post_cols")
+        post_ps = {g: spread(post_cols, (g - OUT_TENSOR) * GROUP) for g in range(OUT_TENSOR, GROUPS)}
+
         t = held.tile([P, N], F32, name="t")
-        pieces = [(0, ROOT), (T_START[1], N)] + [(first, first + WIDE // 2) for first in range(T_START[4], T_START[1], WIDE // 2)]
-        for first, last in pieces:
+        out_blocks = OUT_TENSOR * GROUP
+        early = [(T_START[k], T_START[k] + out_blocks * count) for k, count in ((0, P >> 4), (4, P >> 1), (1, P >> 4))]
+        assert early[1][0] <= T_START[3] and T_START[3] + out_blocks * (P >> 2) <= early[1][1]
+        assert early[1][0] <= T_START[2] and T_START[2] + out_blocks * (P >> 3) <= early[1][1]
+        late = [(early[0][1], early[1][0]), (early[1][1], early[2][0]), (early[2][1], N)]
+        for first, last in early + late:
             nc.vector.tensor_tensor(
                 t[:, first:last], w[:].indirect(offsets[:, first // 16 : last // 16]), mid_sb[:, first:last], MULT
             )
@@ -226,10 +249,15 @@ def tile_waveletlayer_kernel(tc, x, pre, mid, post, offs, out):
                         ADD,
                     )
 
-        def finish(m0, m1):
-            cols = slice(16 * m0, 16 * m1)
+        def finish(g):
+            cols = slice(g * WIDE, (g + 1) * WIDE)
             nc.vector.scalar_tensor_tensor(
-                grouped(o_sb[:, cols], 2), across(halves[4], 2)[:, 8 * m0 : 8 * m1, :], R**4, grouped(post_sb[:, cols], 2), MULT, MULT
+                grouped(o_sb[:, cols], 2),
+                across(halves[4], 2)[:, g * WIDE // 2 : (g + 1) * WIDE // 2, :],
+                R**4,
+                grouped(post_ps[g][:], 2),
+                MULT,
+                MULT,
             )
             nc.sync.dma_start(out[:, cols], o_sb[:, cols])
 
@@ -243,4 +271,4 @@ def tile_waveletlayer_kernel(tc, x, pre, mid, post, offs, out):
                     if behind < 2:
                         double(3 + behind, g * roots, (g + 1) * roots)
                     else:
-                        finish(g * roots, (g + 1) * roots)
+                        finish(g)

import math

import concourse.mybir as mybir
from concourse.masks import make_identity

F32 = mybir.dt.float32
U16 = mybir.dt.uint16
ADD = mybir.AluOpType.add
SUB = mybir.AluOpType.subtract
MULT = mybir.AluOpType.mult
COPY = mybir.ActivationFunctionType.Copy

P = 128
S = 4096
N = 2304
R = math.sqrt(0.5)
ROOT = S // 16
T_START = {0: 0, 1: 2048, 2: 1024, 3: 512, 4: 256}
SIGNS = ((0, 1.0), (1, -1.0))

GROUP = 4
WIDE = GROUP * P
GROUPS = S // WIDE
IN_TENSOR = GROUPS // 2
OUT_TENSOR = GROUPS // 2

FLOPS = P * (2 * S + N + 4 * (S - ROOT))


def grouped(ap, g):
    return ap.rearrange("p (j r) -> p j r", r=g)


def across(ap, runs):
    return ap.rearrange("p (r j) -> p j r", r=runs)


def coefficient_places(n):
    return [(0, n >> 4)] + [(n >> k, n >> k) for k in (4, 3, 2, 1)]


def tile_waveletlayer_kernel(tc, x, pre, mid, post, offs, out):
    nc = tc.nc
    pre_row = pre.rearrange("o n -> (o n)")
    mid_row = mid.rearrange("o n -> (o n)")
    post_row = post.rearrange("o n -> (o n)")
    in_vector = GROUPS - IN_TENSOR
    split = IN_TENSOR * WIDE

    with (
        tc.tile_pool(name="held", bufs=1) as held,
        tc.tile_pool(name="ring", bufs=3) as ring,
        tc.psum_pool(name="psum", bufs=2) as psum,
        tc.psum_pool(name="spreads", bufs=GROUPS - OUT_TENSOR) as spreads,
    ):
        offsets = held.tile([P, N // 16], U16, name="offsets")
        nc.sync.dma_start(offsets[:], offs)
        pre_rows = held.tile([S // P, P], F32, name="pre_rows")
        nc.sync.dma_start(pre_rows[:], pre_row.rearrange("(b s) -> b s", s=P))
        out_split = OUT_TENSOR * WIDE
        post_rows = held.tile([(S - out_split) // P, P], F32, name="post_rows")
        nc.sync.dma_start(post_rows[:], post_row[out_split:S].rearrange("(b s) -> b s", s=P))
        x_sb = held.tile([P, S], F32, name="x_sb")
        for i in range(max(IN_TENSOR, in_vector)):
            if i < IN_TENSOR:
                nc.sync.dma_start(x_sb[:, i * WIDE : (i + 1) * WIDE], x[:, i * WIDE : (i + 1) * WIDE])
            if i < in_vector:
                nc.sync.dma_start(x_sb[:, split + i * WIDE : split + (i + 1) * WIDE], x[:, split + i * WIDE : split + (i + 1) * WIDE])
        mid_sb = held.tile([P, N], F32, name="mid_sb")
        mid_cut = T_START[4] + OUT_TENSOR * WIDE // 2
        for cols in (slice(0, mid_cut), slice(mid_cut, N)):
            nc.sync.dma_start(mid_sb[:, cols], mid_row[cols].partition_broadcast(P))
        post_sb = held.tile([P, out_split], F32, name="post_sb")
        for cols in (slice(0, out_split // 2), slice(out_split // 2, out_split)):
            nc.sync.dma_start(post_sb[:, cols], post_row[cols].partition_broadcast(P))

        identity = held.tile([P, P], F32, name="identity")
        make_identity(nc, identity[:])

        def blocks_to_columns(rows, name):
            blocks = rows.shape[0]
            columns_ps = psum.tile([P, WIDE], F32, name="flipped_ps")
            nc.tensor.matmul(columns_ps[:, 0:blocks], rows, identity[0:blocks, 0:blocks])
            columns = held.tile([P, blocks], F32, name=name)
            nc.scalar.activation(columns[:], columns_ps[:, 0:blocks], COPY)
            return columns

        def spread(columns, first):
            spread_ps = spreads.tile([P, WIDE], F32, name="spread_ps")
            for i in range(GROUP):
                one = columns[:, first + i : first + i + 1]
                nc.tensor.transpose(spread_ps[:, i * P : (i + 1) * P], one.to_broadcast([P, P]), identity[:])
            return spread_ps

        pre_cols = blocks_to_columns(pre_rows[:], "pre_cols")

        haar = held.tile([P, P], F32, name="haar")
        sums = identity
        for k in (1, 2, 3, 4):
            half = P >> k
            two = grouped(sums[:], 2)
            sums = held.tile([P, half], F32, name=f"impulse_sum{k}")
            nc.gpsimd.tensor_tensor(sums[:], two[:, :, 0], two[:, :, 1], ADD)
            diff = held.tile([P, half], F32, name=f"impulse_diff{k}")
            nc.gpsimd.tensor_tensor(diff[:], two[:, :, 0], two[:, :, 1], SUB)
            nc.scalar.mul(haar[:, half : 2 * half], diff[:], R**k)
        nc.scalar.mul(haar[:, 0 : P >> 4], sums[:], R**4)

        w = held.tile([P, S], F32, name="w")
        flipped = {}

        def flip_x(g):
            flipped_ps = psum.tile([P, WIDE], F32, name="flipped_ps")
            flipped[g] = ring.tile([P, WIDE], F32, name="flipped")
            for i in range(GROUP):
                b = g * GROUP + i
                nc.tensor.transpose(flipped_ps[:, i * P : (i + 1) * P], x_sb[:, b * P : (b + 1) * P], identity[:])
            for i in range(GROUP):
                b = g * GROUP + i
                nc.scalar.mul(flipped[g][:, i * P : (i + 1) * P], flipped_ps[:, i * P : (i + 1) * P], pre_cols[:, b : b + 1])

        def analyse_on_tensor(g):
            product_ps = psum.tile([P, WIDE], F32, name="product_ps")
            for i in range(GROUP):
                nc.tensor.matmul(product_ps[:, i * P : (i + 1) * P], flipped[g][:, i * P : (i + 1) * P], haar[:])
            for (in_block, count), in_w in zip(coefficient_places(P), coefficient_places(S)):
                first = in_w[0] + g * GROUP * count
                nc.scalar.activation(
                    grouped(w[:, first : first + GROUP * count], count),
                    grouped(product_ps[:], P)[:, :, in_block : in_block + count],
                    COPY,
                )

        sums = {k: held.tile([P, (S - split) >> k], F32, name=f"sum{k}") for k in (0, 1, 2, 3)}
        diffs = {k: held.tile([P, (S - split) >> k], F32, name=f"diff{k}") for k in (1, 2, 3)}

        def scale(v):
            pre_ps = spread(pre_cols, (IN_TENSOR + v) * GROUP)
            nc.vector.scalar_tensor_tensor(
                across(sums[0][:, v * WIDE : (v + 1) * WIDE], 2),
                grouped(x_sb[:, split + v * WIDE : split + (v + 1) * WIDE], 2),
                R**4,
                grouped(pre_ps[:], 2),
                MULT,
                MULT,
            )

        def halve(k, two_runs, sum_to, first):
            n = two_runs.shape[1] // 2
            even, odd = two_runs[:, 0:n], two_runs[:, n : 2 * n]
            d_k = slice((S >> k) + first, (S >> k) + first + n)
            if k < 4:
                nc.vector.tensor_tensor(sum_to, grouped(even, 2), grouped(odd, 2), ADD)
                here = slice(first - (split >> k), first - (split >> k) + n)
                nc.vector.tensor_tensor(diffs[k][:, here], even, odd, SUB)
                nc.scalar.mul(w[:, d_k], diffs[k][:, here], R ** (k - 4))
            else:
                nc.vector.tensor_tensor(w[:, first : first + n], even, odd, ADD)
                nc.vector.tensor_tensor(w[:, d_k], even, odd, SUB)

        def first_level(v):
            halve(1, sums[0][:, v * WIDE : (v + 1) * WIDE], across(sums[1][:, v * WIDE // 2 : (v + 1) * WIDE // 2], 2), (split + v * WIDE) >> 1)

        def second_level(v):
            rows = slice(v * WIDE // 8, (v + 1) * WIDE // 8)
            halve(2, sums[1][:, v * WIDE // 2 : (v + 1) * WIDE // 2], across(sums[2][:], 2)[:, rows, :], (split + v * WIDE) >> 2)

        for i in range(max(IN_TENSOR, in_vector) + 1):
            if i < in_vector:
                scale(i)
            if i < IN_TENSOR:
                flip_x(i)
            if 0 < i <= IN_TENSOR:
                analyse_on_tensor(i - 1)
            if 0 < i <= in_vector:
                second_level(i - 1)
            if i < in_vector:
                first_level(i)
        halve(3, sums[2][:], across(sums[3][:], 2), split >> 3)
        halve(4, sums[3][:], None, split >> 4)

        haar_flipped_ps = psum.tile([P, WIDE], F32, name="flipped_ps")
        nc.tensor.transpose(haar_flipped_ps[:, 0:P], haar[:], identity[:])
        haar_flipped = held.tile([P, P], F32, name="haar_flipped")
        nc.scalar.activation(haar_flipped[:], haar_flipped_ps[:, 0:P], COPY)

        post_cols = blocks_to_columns(post_rows[:], "post_cols")
        post_ps = {g: spread(post_cols, (g - OUT_TENSOR) * GROUP) for g in range(OUT_TENSOR, GROUPS)}

        t = held.tile([P, N], F32, name="t")
        out_blocks = OUT_TENSOR * GROUP
        early = [(T_START[k], T_START[k] + out_blocks * count) for k, count in ((0, P >> 4), (4, P >> 1), (1, P >> 4))]
        assert early[1][0] <= T_START[3] and T_START[3] + out_blocks * (P >> 2) <= early[1][1]
        assert early[1][0] <= T_START[2] and T_START[2] + out_blocks * (P >> 3) <= early[1][1]
        late = [(early[0][1], early[1][0]), (early[1][1], early[2][0]), (early[2][1], N)]
        for first, last in early + late:
            nc.vector.tensor_tensor(
                t[:, first:last], w[:].indirect(offsets[:, first // 16 : last // 16]), mid_sb[:, first:last], MULT
            )

        o_sb = held.tile([P, S], F32, name="o_sb")

        def flip_t(g):
            packed = ring.tile([P, WIDE], F32, name="packed")
            for k, (in_block, count) in enumerate(coefficient_places(P)):
                first = T_START[k] + g * GROUP * count
                nc.scalar.activation(
                    grouped(packed[:], P)[:, :, in_block : in_block + count],
                    grouped(t[:, first : first + GROUP * count], count),
                    COPY,
                )
            flipped_ps = psum.tile([P, WIDE], F32, name="flipped_ps")
            for i in range(GROUP):
                nc.tensor.transpose(flipped_ps[:, i * P : (i + 1) * P], packed[:, i * P : (i + 1) * P], identity[:])
            flipped[g] = ring.tile([P, WIDE], F32, name="flipped")
            nc.scalar.activation(flipped[g][:], flipped_ps[:], COPY)

        def synthesise_on_tensor(g):
            product_ps = psum.tile([P, WIDE], F32, name="product_ps")
            for i in range(GROUP):
                nc.tensor.matmul(product_ps[:, i * P : (i + 1) * P], flipped[g][:, i * P : (i + 1) * P], haar_flipped[:])
            cols = slice(g * WIDE, (g + 1) * WIDE)
            nc.vector.tensor_tensor(o_sb[:, cols], product_ps[:], post_sb[:, cols], MULT)
            nc.sync.dma_start(out[:, cols], o_sb[:, cols])

        flip_t(0)
        for g in range(OUT_TENSOR):
            if g + 1 < OUT_TENSOR:
                flip_t(g + 1)
            synthesise_on_tensor(g)

        halves = {k: held.tile([P, ROOT << k], F32, name=f"halves{k}") for k in (1, 2, 3, 4)}

        def double(k, m0, m1):
            g = 1 << (k - 1)
            n = ROOT * g
            f_k = t[:, T_START[k] + g * m0 : T_START[k] + g * m1]
            for s, sign in SIGNS:
                run = halves[k][:, s * n + g * m0 : s * n + g * m1]
                if k == 1:
                    nc.vector.scalar_tensor_tensor(run, f_k, sign, t[:, m0:m1], MULT, ADD)
                else:
                    nc.vector.scalar_tensor_tensor(
                        grouped(run, 2),
                        grouped(f_k, 2),
                        sign * R ** (1 - k),
                        across(halves[k - 1], 2)[:, g * m0 // 2 : g * m1 // 2, :],
                        MULT,
                        ADD,
                    )

        def finish(g):
            cols = slice(g * WIDE, (g + 1) * WIDE)
            nc.vector.scalar_tensor_tensor(
                grouped(o_sb[:, cols], 2),
                across(halves[4], 2)[:, g * WIDE // 2 : (g + 1) * WIDE // 2, :],
                R**4,
                grouped(post_ps[g][:], 2),
                MULT,
                MULT,
            )
            nc.sync.dma_start(out[:, cols], o_sb[:, cols])

        roots = WIDE // 16
        double(1, OUT_TENSOR * roots, ROOT)
        double(2, OUT_TENSOR * roots, ROOT)
        for step in range(OUT_TENSOR, GROUPS + 2):
            for behind in range(3):
                g = step - behind
                if OUT_TENSOR <= g < GROUPS:
                    if behind < 2:
                        double(3 + behind, g * roots, (g + 1) * roots)
                    else:
                        finish(g)
